import numpy as np
import ml_dtypes

BF16 = ml_dtypes.bfloat16


def bf(x):
    return np.asarray(x, np.float32).astype(BF16)


def f32(x):
    return np.asarray(x, np.float32)


def f64(x):
    return np.asarray(x).astype(np.float64)


def striped(idx):
    return np.tile(idx.reshape(-1, 16).T, (8, 1))


SEQ, LOBS, T, HID, C, S, N, K = 2, 3, 4, 128, 1024, 256, 1024, 4


def setup_inputs():
    table = f32(0.5 * np.random.standard_normal((C, S)))
    obs = f32(np.random.standard_normal((SEQ * LOBS, N)))
    pattern = np.random.permutation(N) % (SEQ + 1)
    mask = f32(pattern[None, :] == np.arange(SEQ)[:, None])
    idx = np.concatenate([np.random.permutation(S) for _ in range(K)])
    return {"table": table, "obs": obs, "mask": mask, "offs": striped(idx)}


def reference(table, obs, mask, offs):
    idx = offs[:16].T.reshape(-1)
    picked = f64(table)[:, idx].reshape(SEQ, T, HID, N)
    o = f64(obs).reshape(SEQ, LOBS, 1, N)
    limb = (picked[:, :LOBS] * o).sum(axis=1) + picked[:, LOBS]
    keep = 1.0 - f64(mask).reshape(SEQ, 1, N)
    return np.maximum((limb * keep).sum(axis=0), 0.0)

@@ -1,0 +1,68 @@
+import concourse.mybir as mybir
+
+F32 = mybir.dt.float32
+U16 = mybir.dt.uint16
+MULT = mybir.AluOpType.mult
+ADD = mybir.AluOpType.add
+
+P = 128
+ROBOTS = 256
+N = 1024
+LIMBS = 2
+FEATURES = 3
+BLOCKS = LIMBS * (FEATURES + 1)
+PIECE = 256
+PIECE_COLS = PIECE // 16
+
+
+def tile_mlpmodel_kernel(tc, table, obs, mask, offs, out):
+    nc = tc.nc
+    with (
+        tc.tile_pool(name="held", bufs=1) as held,
+        tc.tile_pool(name="work", bufs=3) as work,
+    ):
+        offsets = held.tile([P, N // 16], U16, name="offsets")
+        nc.sync.dma_start(offsets[:], offs)
+
+        blocks = [held.tile([P, ROBOTS], F32, name=f"block{b}") for b in range(BLOCKS)]
+        for b in range(BLOCKS):
+            nc.scalar.dma_start(blocks[b][:], table[b * P : (b + 1) * P, :])
+
+        mask_all = [held.tile([P, N], F32, name=f"mask_all{s}") for s in range(LIMBS)]
+        obs_all = [held.tile([P, N], F32, name=f"obs_all{r}") for r in range(LIMBS * FEATURES)]
+        for s in range(LIMBS):
+            for i in range(FEATURES):
+                r = FEATURES * s + i
+                nc.sync.dma_start(obs_all[r][:], obs[r, :].partition_broadcast(P))
+            nc.sync.dma_start(mask_all[s][:], mask[s, :].partition_broadcast(P))
+
+        keep_all = [held.tile([P, N], F32, name=f"keep_all{s}") for s in range(LIMBS)]
+        for s in range(LIMBS):
+            nc.vector.tensor_scalar(keep_all[s][:], mask_all[s][:], -1.0, 1.0, MULT, ADD)
+
+        for p in range(N // PIECE):
+            cols = slice(p * PIECE, (p + 1) * PIECE)
+            piece = offsets[:, p * PIECE_COLS : (p + 1) * PIECE_COLS]
+            limbs = []
+            for s in range(LIMBS):
+                first = (FEATURES + 1) * s
+                limb = work.tile([P, PIECE], F32, name=f"limb{s}")
+                nc.vector.tensor_tensor(
+                    limb[:], blocks[first][:].indirect(piece), obs_all[FEATURES * s][:, cols], MULT
+                )
+                for i in range(1, FEATURES):
+                    term = work.tile([P, PIECE], F32, name="term")
+                    nc.vector.tensor_tensor(
+                        term[:], blocks[first + i][:].indirect(piece), obs_all[FEATURES * s + i][:, cols], MULT
+                    )
+                    nc.vector.tensor_tensor(limb[:], limb[:], term[:], ADD)
+                biased = work.tile([P, PIECE], F32, name=f"biased{s}")
+                nc.vector.tensor_tensor(
+                    biased[:], blocks[first + FEATURES][:].indirect(piece), limb[:], ADD
+                )
+                nc.vector.tensor_tensor(biased[:], biased[:], keep_all[s][:, cols], MULT)
+                limbs.append(biased)
+            result = work.tile([P, PIECE], F32, name="result")
+            nc.vector.tensor_tensor(result[:], limbs[0][:], limbs[1][:], ADD)
+            nc.vector.tensor_scalar_max(result[:], result[:], 0.0)
+            nc.sync.dma_start(out[:, cols], result[:])

@@ -1,17 +1,20 @@
 import concourse.mybir as mybir
+from concourse.masks import make_identity
 
 F32 = mybir.dt.float32
 U16 = mybir.dt.uint16
 MULT = mybir.AluOpType.mult
-ADD = mybir.AluOpType.add
+COPY = mybir.ActivationFunctionType.Copy
+RELU = mybir.ActivationFunctionType.Relu
 
 P = 128
 ROBOTS = 256
 N = 1024
 LIMBS = 2
 FEATURES = 3
-BLOCKS = LIMBS * (FEATURES + 1)
+PER_LIMB = FEATURES + 1
 PIECE = 256
+PIECES = N // PIECE
 PIECE_COLS = PIECE // 16
 
 
@@ -19,50 +22,59 @@ def tile_mlpmodel_kernel(tc, table, obs, mask, offs, out):
     nc = tc.nc
     with (
         tc.tile_pool(name="held", bufs=1) as held,
-        tc.tile_pool(name="work", bufs=3) as work,
+        tc.tile_pool(name="ring", bufs=6) as ring,
+        tc.psum_pool(name="psum", bufs=1) as psum,
     ):
         offsets = held.tile([P, N // 16], U16, name="offsets")
         nc.sync.dma_start(offsets[:], offs)
 
-        blocks = [held.tile([P, ROBOTS], F32, name=f"block{b}") for b in range(BLOCKS)]
-        for b in range(BLOCKS):
+        bias_blocks = [PER_LIMB * s + FEATURES for s in range(LIMBS)]
+        weight_blocks = [PER_LIMB * s + i for s in range(LIMBS) for i in range(FEATURES)]
+        order = bias_blocks + weight_blocks
+
+        blocks = {}
+        for b in order:
+            blocks[b] = held.tile([P, ROBOTS], F32, name=f"block{b}")
             nc.scalar.dma_start(blocks[b][:], table[b * P : (b + 1) * P, :])
 
         mask_all = [held.tile([P, N], F32, name=f"mask_all{s}") for s in range(LIMBS)]
         obs_all = [held.tile([P, N], F32, name=f"obs_all{r}") for r in range(LIMBS * FEATURES)]
         for s in range(LIMBS):
-            for i in range(FEATURES):
-                r = FEATURES * s + i
-                nc.sync.dma_start(obs_all[r][:], obs[r, :].partition_broadcast(P))
             nc.sync.dma_start(mask_all[s][:], mask[s, :].partition_broadcast(P))
+        for r in range(LIMBS * FEATURES):
+            nc.sync.dma_start(obs_all[r][:], obs[r, :].partition_broadcast(P))
 
-        keep_all = [held.tile([P, N], F32, name=f"keep_all{s}") for s in range(LIMBS)]
+        identity = held.tile([P, P], F32, name="identity")
+        make_identity(nc, identity[:])
+
+        factor = {}
         for s in range(LIMBS):
-            nc.vector.tensor_scalar(keep_all[s][:], mask_all[s][:], -1.0, 1.0, MULT, ADD)
+            keep = held.tile([P, N], F32, name=f"keep{s}")
+            for p in range(PIECES):
+                cols = slice(p * PIECE, (p + 1) * PIECE)
+                nc.scalar.activation(keep[:, cols], mask_all[s][:, cols], COPY, bias=1.0, scale=-1.0)
+            factor[PER_LIMB * s + FEATURES] = keep
+        for s in range(LIMBS):
+            for i in range(FEATURES):
+                kept_obs = held.tile([P, N], F32, name=f"kept_obs{FEATURES * s + i}")
+                nc.gpsimd.tensor_tensor(
+                    kept_obs[:], obs_all[FEATURES * s + i][:], factor[PER_LIMB * s + FEATURES][:], MULT
+                )
+                factor[PER_LIMB * s + i] = kept_obs
 
-        for p in range(N // PIECE):
+        sums = [psum.tile([P, PIECE], F32, name=f"sum{p}") for p in range(PIECES)]
+        for k, b in enumerate(order):
+            for p in range(PIECES):
+                cols = slice(p * PIECE, (p + 1) * PIECE)
+                piece = offsets[:, p * PIECE_COLS : (p + 1) * PIECE_COLS]
+                product = ring.tile([P, PIECE], F32, name="product")
+                nc.vector.tensor_tensor(product[:], blocks[b][:].indirect(piece), factor[b][:, cols], MULT)
+                nc.tensor.matmul(
+                    sums[p][:], identity[:], product[:], start=(k == 0), stop=(k == len(order) - 1)
+                )
+
+        for p in range(PIECES):
             cols = slice(p * PIECE, (p + 1) * PIECE)
-            piece = offsets[:, p * PIECE_COLS : (p + 1) * PIECE_COLS]
-            limbs = []
-            for s in range(LIMBS):
-                first = (FEATURES + 1) * s
-                limb = work.tile([P, PIECE], F32, name=f"limb{s}")
-                nc.vector.tensor_tensor(
-                    limb[:], blocks[first][:].indirect(piece), obs_all[FEATURES * s][:, cols], MULT
-                )
-                for i in range(1, FEATURES):
-                    term = work.tile([P, PIECE], F32, name="term")
-                    nc.vector.tensor_tensor(
-                        term[:], blocks[first + i][:].indirect(piece), obs_all[FEATURES * s + i][:, cols], MULT
-                    )
-                    nc.vector.tensor_tensor(limb[:], limb[:], term[:], ADD)
-                biased = work.tile([P, PIECE], F32, name=f"biased{s}")
-                nc.vector.tensor_tensor(
-                    biased[:], blocks[first + FEATURES][:].indirect(piece), limb[:], ADD
-                )
-                nc.vector.tensor_tensor(biased[:], biased[:], keep_all[s][:, cols], MULT)
-                limbs.append(biased)
-            result = work.tile([P, PIECE], F32, name="result")
-            nc.vector.tensor_tensor(result[:], limbs[0][:], limbs[1][:], ADD)
-            nc.vector.tensor_scalar_max(result[:], result[:], 0.0)
+            result = ring.tile([P, PIECE], F32, name="result")
+            nc.scalar.activation(result[:], sums[p][:], RELU)
             nc.sync.dma_start(out[:, cols], result[:])

@@ -4,6 +4,7 @@ from concourse.masks import make_identity
 F32 = mybir.dt.float32
 U16 = mybir.dt.uint16
 MULT = mybir.AluOpType.mult
+ADD = mybir.AluOpType.add
 COPY = mybir.ActivationFunctionType.Copy
 RELU = mybir.ActivationFunctionType.Relu
 
@@ -16,6 +17,8 @@ PER_LIMB = FEATURES + 1
 PIECE = 256
 PIECES = N // PIECE
 PIECE_COLS = PIECE // 16
+CHUNKS = 16
+CHUNK = N // CHUNKS
 
 
 def tile_mlpmodel_kernel(tc, table, obs, mask, offs, out):
@@ -28,24 +31,51 @@ def tile_mlpmodel_kernel(tc, table, obs, mask, offs, out):
         offsets = held.tile([P, N // 16], U16, name="offsets")
         nc.sync.dma_start(offsets[:], offs)
 
+        mask_small = held.tile([LIMBS * CHUNKS, CHUNK], F32, name="mask_small")
+        obs_small = held.tile([LIMBS * CHUNKS, FEATURES, CHUNK], F32, name="obs_small")
+        nc.sync.dma_start(mask_small[:], mask.rearrange("s (c x) -> (s c) x", c=CHUNKS))
+        for s in range(LIMBS):
+            nc.sync.dma_start(
+                obs_small[s * CHUNKS : (s + 1) * CHUNKS, :, :],
+                obs[s * FEATURES : (s + 1) * FEATURES, :].rearrange("i (c x) -> c i x", c=CHUNKS),
+            )
+
         bias_blocks = [PER_LIMB * s + FEATURES for s in range(LIMBS)]
         weight_blocks = [PER_LIMB * s + i for s in range(LIMBS) for i in range(FEATURES)]
         order = bias_blocks + weight_blocks
 
-        blocks = {}
-        for b in order:
-            blocks[b] = held.tile([P, ROBOTS], F32, name=f"block{b}")
-            nc.scalar.dma_start(blocks[b][:], table[b * P : (b + 1) * P, :])
-
+        blocks = {b: held.tile([P, ROBOTS], F32, name=f"block{b}") for b in order}
         mask_all = [held.tile([P, N], F32, name=f"mask_all{s}") for s in range(LIMBS)]
-        obs_all = [held.tile([P, N], F32, name=f"obs_all{r}") for r in range(LIMBS * FEATURES)]
         for s in range(LIMBS):
-            nc.sync.dma_start(mask_all[s][:], mask[s, :].partition_broadcast(P))
-        for r in range(LIMBS * FEATURES):
-            nc.sync.dma_start(obs_all[r][:], obs[r, :].partition_broadcast(P))
+            b = bias_blocks[s]
+            nc.sync.dma_start(blocks[b][:], table[b * P : (b + 1) * P, :])
+            for p in range(PIECES):
+                cols = slice(p * PIECE, (p + 1) * PIECE)
+                nc.sync.dma_start(mask_all[s][:, cols], mask[s, cols].partition_broadcast(P))
+        for b in weight_blocks:
+            nc.sync.dma_start(blocks[b][:], table[b * P : (b + 1) * P, :])
 
         identity = held.tile([P, P], F32, name="identity")
         make_identity(nc, identity[:])
+
+        warm = held.tile([P, 1], F32, name="warm")
+        nc.scalar.activation(warm[:], identity[:, 0:1], COPY)
+
+        keep_small = held.tile([LIMBS * CHUNKS, CHUNK], F32, name="keep_small")
+        kept_small = held.tile([LIMBS * CHUNKS, FEATURES, CHUNK], F32, name="kept_small")
+        nc.vector.tensor_scalar(keep_small[:], mask_small[:], -1.0, 1.0, MULT, ADD)
+        nc.vector.tensor_tensor(
+            kept_small[:],
+            obs_small[:],
+            keep_small[:].unsqueeze(1).to_broadcast([LIMBS * CHUNKS, FEATURES, CHUNK]),
+            MULT,
+        )
+
+        for s in range(LIMBS):
+            nc.sync.dma_start(
+                out[s * FEATURES : (s + 1) * FEATURES, :].rearrange("i (c x) -> c i x", c=CHUNKS),
+                kept_small[s * CHUNKS : (s + 1) * CHUNKS, :, :],
+            )
 
         factor = {}
         for s in range(LIMBS):
@@ -53,14 +83,11 @@ def tile_mlpmodel_kernel(tc, table, obs, mask, offs, out):
             for p in range(PIECES):
                 cols = slice(p * PIECE, (p + 1) * PIECE)
                 nc.scalar.activation(keep[:, cols], mask_all[s][:, cols], COPY, bias=1.0, scale=-1.0)
-            factor[PER_LIMB * s + FEATURES] = keep
-        for s in range(LIMBS):
-            for i in range(FEATURES):
-                kept_obs = held.tile([P, N], F32, name=f"kept_obs{FEATURES * s + i}")
-                nc.gpsimd.tensor_tensor(
-                    kept_obs[:], obs_all[FEATURES * s + i][:], factor[PER_LIMB * s + FEATURES][:], MULT
-                )
-                factor[PER_LIMB * s + i] = kept_obs
+            factor[bias_blocks[s]] = keep
+        for r, b in enumerate(weight_blocks):
+            kept_obs = held.tile([P, N], F32, name=f"kept_obs{r}")
+            nc.sync.dma_start(kept_obs[:], out[r, :].partition_broadcast(P))
+            factor[b] = kept_obs
 
         sums = [psum.tile([P, PIECE], F32, name=f"sum{p}") for p in range(PIECES)]
         for k, b in enumerate(order):

@@ -28,9 +28,6 @@ def tile_mlpmodel_kernel(tc, table, obs, mask, offs, out):
         tc.tile_pool(name="ring", bufs=6) as ring,
         tc.psum_pool(name="psum", bufs=1) as psum,
     ):
-        offsets = held.tile([P, N // 16], U16, name="offsets")
-        nc.sync.dma_start(offsets[:], offs)
-
         mask_small = held.tile([LIMBS * CHUNKS, CHUNK], F32, name="mask_small")
         obs_small = held.tile([LIMBS * CHUNKS, FEATURES, CHUNK], F32, name="obs_small")
         nc.sync.dma_start(mask_small[:], mask.rearrange("s (c x) -> (s c) x", c=CHUNKS))
@@ -40,6 +37,9 @@ def tile_mlpmodel_kernel(tc, table, obs, mask, offs, out):
                 obs[s * FEATURES : (s + 1) * FEATURES, :].rearrange("i (c x) -> c i x", c=CHUNKS),
             )
 
+        offsets = held.tile([P, N // 16], U16, name="offsets")
+        nc.sync.dma_start(offsets[:], offs)
+
         bias_blocks = [PER_LIMB * s + FEATURES for s in range(LIMBS)]
         weight_blocks = [PER_LIMB * s + i for s in range(LIMBS) for i in range(FEATURES)]
         order = bias_blocks + weight_blocks
@@ -48,15 +48,15 @@ def tile_mlpmodel_kernel(tc, table, obs, mask, offs, out):
         mask_all = [held.tile([P, N], F32, name=f"mask_all{s}") for s in range(LIMBS)]
         for s in range(LIMBS):
             b = bias_blocks[s]
-            nc.sync.dma_start(blocks[b][:], table[b * P : (b + 1) * P, :])
+            nc.scalar.dma_start(blocks[b][:], table[b * P : (b + 1) * P, :])
             for p in range(PIECES):
                 cols = slice(p * PIECE, (p + 1) * PIECE)
-                nc.sync.dma_start(mask_all[s][:, cols], mask[s, cols].partition_broadcast(P))
-        for b in weight_blocks:
-            nc.sync.dma_start(blocks[b][:], table[b * P : (b + 1) * P, :])
+                nc.scalar.dma_start(mask_all[s][:, cols], mask[s, cols].partition_broadcast(P))
 
         identity = held.tile([P, P], F32, name="identity")
         make_identity(nc, identity[:])
+        for b in weight_blocks:
+            nc.gpsimd.dma_start(blocks[b][:], table[b * P : (b + 1) * P, :])
 
         warm = held.tile([P, 1], F32, name="warm")
         nc.scalar.activation(warm[:], identity[:, 0:1], COPY)
@@ -86,7 +86,9 @@ def tile_mlpmodel_kernel(tc, table, obs, mask, offs, out):
             factor[bias_blocks[s]] = keep
         for r, b in enumerate(weight_blocks):
             kept_obs = held.tile([P, N], F32, name=f"kept_obs{r}")
-            nc.sync.dma_start(kept_obs[:], out[r, :].partition_broadcast(P))
+            for p in range(PIECES):
+                cols = slice(p * PIECE, (p + 1) * PIECE)
+                nc.sync.dma_start(kept_obs[:, cols], out[r, cols].partition_broadcast(P))
             factor[b] = kept_obs
 
         sums = [psum.tile([P, PIECE], F32, name=f"sum{p}") for p in range(PIECES)]

@@ -28,6 +28,20 @@ def tile_mlpmodel_kernel(tc, table, obs, mask, offs, out):
         tc.tile_pool(name="ring", bufs=6) as ring,
         tc.psum_pool(name="psum", bufs=1) as psum,
     ):
+        bias_blocks = [PER_LIMB * s + FEATURES for s in range(LIMBS)]
+        weight_blocks = [PER_LIMB * s + i for s in range(LIMBS) for i in range(FEATURES)]
+        order = bias_blocks + weight_blocks
+
+        blocks = {b: held.tile([P, ROBOTS], F32, name=f"block{b}") for b in order}
+        mask_all = [held.tile([P, N], F32, name=f"mask_all{s}") for s in range(LIMBS)]
+
+        def load_bias_block_and_mask(s):
+            b = bias_blocks[s]
+            nc.sync.dma_start(blocks[b][:], table[b * P : (b + 1) * P, :])
+            for p in range(PIECES):
+                cols = slice(p * PIECE, (p + 1) * PIECE)
+                nc.sync.dma_start(mask_all[s][:, cols], mask[s, cols].partition_broadcast(P))
+
         mask_small = held.tile([LIMBS * CHUNKS, CHUNK], F32, name="mask_small")
         obs_small = held.tile([LIMBS * CHUNKS, FEATURES, CHUNK], F32, name="obs_small")
         nc.sync.dma_start(mask_small[:], mask.rearrange("s (c x) -> (s c) x", c=CHUNKS))
@@ -39,24 +53,10 @@ def tile_mlpmodel_kernel(tc, table, obs, mask, offs, out):
 
         offsets = held.tile([P, N // 16], U16, name="offsets")
         nc.sync.dma_start(offsets[:], offs)
-
-        bias_blocks = [PER_LIMB * s + FEATURES for s in range(LIMBS)]
-        weight_blocks = [PER_LIMB * s + i for s in range(LIMBS) for i in range(FEATURES)]
-        order = bias_blocks + weight_blocks
-
-        blocks = {b: held.tile([P, ROBOTS], F32, name=f"block{b}") for b in order}
-        mask_all = [held.tile([P, N], F32, name=f"mask_all{s}") for s in range(LIMBS)]
-        for s in range(LIMBS):
-            b = bias_blocks[s]
-            nc.scalar.dma_start(blocks[b][:], table[b * P : (b + 1) * P, :])
-            for p in range(PIECES):
-                cols = slice(p * PIECE, (p + 1) * PIECE)
-                nc.scalar.dma_start(mask_all[s][:, cols], mask[s, cols].partition_broadcast(P))
+        load_bias_block_and_mask(0)
 
         identity = held.tile([P, P], F32, name="identity")
         make_identity(nc, identity[:])
-        for b in weight_blocks:
-            nc.gpsimd.dma_start(blocks[b][:], table[b * P : (b + 1) * P, :])
 
         warm = held.tile([P, 1], F32, name="warm")
         nc.scalar.activation(warm[:], identity[:, 0:1], COPY)
@@ -77,6 +77,10 @@ def tile_mlpmodel_kernel(tc, table, obs, mask, offs, out):
                 kept_small[s * CHUNKS : (s + 1) * CHUNKS, :, :],
             )
 
+        load_bias_block_and_mask(1)
+        for b in weight_blocks:
+            nc.sync.dma_start(blocks[b][:], table[b * P : (b + 1) * P, :])
+
         factor = {}
         for s in range(LIMBS):
             keep = held.tile([P, N], F32, name=f"keep{s}")
@@ -86,9 +90,7 @@ def tile_mlpmodel_kernel(tc, table, obs, mask, offs, out):
             factor[bias_blocks[s]] = keep
         for r, b in enumerate(weight_blocks):
             kept_obs = held.tile([P, N], F32, name=f"kept_obs{r}")
-            for p in range(PIECES):
-                cols = slice(p * PIECE, (p + 1) * PIECE)
-                nc.sync.dma_start(kept_obs[:, cols], out[r, cols].partition_broadcast(P))
+            nc.sync.dma_start(kept_obs[:], out[r, :].partition_broadcast(P))
             factor[b] = kept_obs
 
         sums = [psum.tile([P, PIECE], F32, name=f"sum{p}") for p in range(PIECES)]

@@ -2,6 +2,7 @@ import concourse.mybir as mybir
 from concourse.masks import make_identity
 
 F32 = mybir.dt.float32
+BF16 = mybir.dt.bfloat16
 U16 = mybir.dt.uint16
 MULT = mybir.AluOpType.mult
 ADD = mybir.AluOpType.add
@@ -19,6 +20,7 @@ PIECES = N // PIECE
 PIECE_COLS = PIECE // 16
 CHUNKS = 16
 CHUNK = N // CHUNKS
+ROW_TILE = 32
 
 
 def tile_mlpmodel_kernel(tc, table, obs, mask, offs, out):
@@ -33,14 +35,6 @@ def tile_mlpmodel_kernel(tc, table, obs, mask, offs, out):
         order = bias_blocks + weight_blocks
 
         blocks = {b: held.tile([P, ROBOTS], F32, name=f"block{b}") for b in order}
-        mask_all = [held.tile([P, N], F32, name=f"mask_all{s}") for s in range(LIMBS)]
-
-        def load_bias_block_and_mask(s):
-            b = bias_blocks[s]
-            nc.sync.dma_start(blocks[b][:], table[b * P : (b + 1) * P, :])
-            for p in range(PIECES):
-                cols = slice(p * PIECE, (p + 1) * PIECE)
-                nc.sync.dma_start(mask_all[s][:, cols], mask[s, cols].partition_broadcast(P))
 
         mask_small = held.tile([LIMBS * CHUNKS, CHUNK], F32, name="mask_small")
         obs_small = held.tile([LIMBS * CHUNKS, FEATURES, CHUNK], F32, name="obs_small")
@@ -51,15 +45,24 @@ def tile_mlpmodel_kernel(tc, table, obs, mask, offs, out):
                 obs[s * FEATURES : (s + 1) * FEATURES, :].rearrange("i (c x) -> c i x", c=CHUNKS),
             )
 
+        mask_pieces = held.tile([LIMBS * PIECES, PIECE], F32, name="mask_pieces")
+        nc.sync.dma_start(mask_pieces[:], mask.rearrange("s (p x) -> (s p) x", p=PIECES))
+
         offsets = held.tile([P, N // 16], U16, name="offsets")
         nc.sync.dma_start(offsets[:], offs)
-        load_bias_block_and_mask(0)
+        for b in bias_blocks:
+            nc.sync.dma_start(blocks[b][:], table[b * P : (b + 1) * P, :])
 
         identity = held.tile([P, P], F32, name="identity")
         make_identity(nc, identity[:])
 
         warm = held.tile([P, 1], F32, name="warm")
         nc.scalar.activation(warm[:], identity[:, 0:1], COPY)
+
+        pick = held.tile([ROW_TILE, LIMBS * PIECES], BF16, name="pick")
+        nc.vector.tensor_copy(pick[:], identity[0:ROW_TILE, 0 : LIMBS * PIECES])
+        keep_pieces = held.tile([ROW_TILE, PIECE], BF16, name="keep_pieces")
+        nc.vector.memset(keep_pieces[:], 0.0)
 
         keep_small = held.tile([LIMBS * CHUNKS, CHUNK], F32, name="keep_small")
         kept_small = held.tile([LIMBS * CHUNKS, FEATURES, CHUNK], F32, name="kept_small")
@@ -70,6 +73,7 @@ def tile_mlpmodel_kernel(tc, table, obs, mask, offs, out):
             keep_small[:].unsqueeze(1).to_broadcast([LIMBS * CHUNKS, FEATURES, CHUNK]),
             MULT,
         )
+        nc.vector.tensor_scalar(keep_pieces[0 : LIMBS * PIECES, :], mask_pieces[:], -1.0, 1.0, MULT, ADD)
 
         for s in range(LIMBS):
             nc.sync.dma_start(
@@ -77,16 +81,26 @@ def tile_mlpmodel_kernel(tc, table, obs, mask, offs, out):
                 kept_small[s * CHUNKS : (s + 1) * CHUNKS, :, :],
             )
 
-        load_bias_block_and_mask(1)
         for b in weight_blocks:
             nc.sync.dma_start(blocks[b][:], table[b * P : (b + 1) * P, :])
 
         factor = {}
+        spread = [psum.tile([P, 2 * PIECE], F32, name=f"spread{t}") for t in range(LIMBS * PIECES // 2)]
+        for q in range(LIMBS * PIECES):
+            nc.tensor.matmul(
+                spread[q // 2][:, (q % 2) * PIECE : (q % 2 + 1) * PIECE],
+                pick[:, q : q + 1].to_broadcast([ROW_TILE, P]),
+                keep_pieces[:],
+            )
         for s in range(LIMBS):
             keep = held.tile([P, N], F32, name=f"keep{s}")
             for p in range(PIECES):
-                cols = slice(p * PIECE, (p + 1) * PIECE)
-                nc.scalar.activation(keep[:, cols], mask_all[s][:, cols], COPY, bias=1.0, scale=-1.0)
+                q = s * PIECES + p
+                nc.scalar.activation(
+                    keep[:, p * PIECE : (p + 1) * PIECE],
+                    spread[q // 2][:, (q % 2) * PIECE : (q % 2 + 1) * PIECE],
+                    COPY,
+                )
             factor[bias_blocks[s]] = keep
         for r, b in enumerate(weight_blocks):
             kept_obs = held.tile([P, N], F32, name=f"kept_obs{r}")

@@ -6,6 +6,7 @@ BF16 = mybir.dt.bfloat16
 U16 = mybir.dt.uint16
 MULT = mybir.AluOpType.mult
 ADD = mybir.AluOpType.add
+IS_EQUAL = mybir.AluOpType.is_equal
 COPY = mybir.ActivationFunctionType.Copy
 RELU = mybir.ActivationFunctionType.Relu
 
@@ -20,7 +21,6 @@ PIECES = N // PIECE
 PIECE_COLS = PIECE // 16
 CHUNKS = 16
 CHUNK = N // CHUNKS
-ROW_TILE = 32
 
 
 def tile_mlpmodel_kernel(tc, table, obs, mask, offs, out):
@@ -59,18 +59,18 @@ def tile_mlpmodel_kernel(tc, table, obs, mask, offs, out):
         warm = held.tile([P, 1], F32, name="warm")
         nc.scalar.activation(warm[:], identity[:, 0:1], COPY)
 
-        pick = held.tile([ROW_TILE, LIMBS * PIECES], BF16, name="pick")
-        nc.vector.tensor_copy(pick[:], identity[0:ROW_TILE, 0 : LIMBS * PIECES])
-        keep_pieces = held.tile([ROW_TILE, PIECE], BF16, name="keep_pieces")
+        pick = held.tile([P, LIMBS * PIECES], BF16, name="pick")
+        nc.vector.tensor_copy(pick[:], identity[:, 0 : LIMBS * PIECES])
+        keep_pieces = held.tile([P, PIECE], BF16, name="keep_pieces")
         nc.vector.memset(keep_pieces[:], 0.0)
 
-        keep_small = held.tile([LIMBS * CHUNKS, CHUNK], F32, name="keep_small")
         kept_small = held.tile([LIMBS * CHUNKS, FEATURES, CHUNK], F32, name="kept_small")
-        nc.vector.tensor_scalar(keep_small[:], mask_small[:], -1.0, 1.0, MULT, ADD)
-        nc.vector.tensor_tensor(
+        nc.vector.scalar_tensor_tensor(
             kept_small[:],
+            mask_small[:].unsqueeze(1).to_broadcast([LIMBS * CHUNKS, FEATURES, CHUNK]),
+            0.0,
             obs_small[:],
-            keep_small[:].unsqueeze(1).to_broadcast([LIMBS * CHUNKS, FEATURES, CHUNK]),
+            IS_EQUAL,
             MULT,
         )
         nc.vector.tensor_scalar(keep_pieces[0 : LIMBS * PIECES, :], mask_pieces[:], -1.0, 1.0, MULT, ADD)
@@ -89,7 +89,7 @@ def tile_mlpmodel_kernel(tc, table, obs, mask, offs, out):
         for q in range(LIMBS * PIECES):
             nc.tensor.matmul(
                 spread[q // 2][:, (q % 2) * PIECE : (q % 2 + 1) * PIECE],
-                pick[:, q : q + 1].to_broadcast([ROW_TILE, P]),
+                pick[:, q : q + 1].to_broadcast([P, P]),
                 keep_pieces[:],
             )
         for s in range(LIMBS):

@@ -27,7 +27,7 @@ def tile_mlpmodel_kernel(tc, table, obs, mask, offs, out):
     nc = tc.nc
     with (
         tc.tile_pool(name="held", bufs=1) as held,
-        tc.tile_pool(name="ring", bufs=6) as ring,
+        tc.tile_pool(name="ring", bufs=LIMBS * PER_LIMB * PIECES) as ring,
         tc.psum_pool(name="psum", bufs=1) as psum,
     ):
         bias_blocks = [PER_LIMB * s + FEATURES for s in range(LIMBS)]

@@ -107,6 +107,7 @@ def tile_mlpmodel_kernel(tc, table, obs, mask, offs, out):
             nc.sync.dma_start(kept_obs[:], out[r, :].partition_broadcast(P))
             factor[b] = kept_obs
 
+        last_block, last_piece = len(order) - 1, PIECES - 1
         sums = [psum.tile([P, PIECE], F32, name=f"sum{p}") for p in range(PIECES)]
         for k, b in enumerate(order):
             for p in range(PIECES):
@@ -114,12 +115,21 @@ def tile_mlpmodel_kernel(tc, table, obs, mask, offs, out):
                 piece = offsets[:, p * PIECE_COLS : (p + 1) * PIECE_COLS]
                 product = ring.tile([P, PIECE], F32, name="product")
                 nc.vector.tensor_tensor(product[:], blocks[b][:].indirect(piece), factor[b][:, cols], MULT)
-                nc.tensor.matmul(
-                    sums[p][:], identity[:], product[:], start=(k == 0), stop=(k == len(order) - 1)
-                )
+                if p < last_piece:
+                    nc.tensor.matmul(sums[p][:], identity[:], product[:], start=(k == 0), stop=(k == last_block))
+                elif k < last_block:
+                    nc.tensor.matmul(
+                        sums[p][:], identity[:], product[:], start=(k == 0), stop=(k == last_block - 1)
+                    )
+                else:
+                    total = ring.tile([P, PIECE], F32, name="total")
+                    nc.vector.tensor_tensor(total[:], product[:], sums[p][:], ADD)
 
         for p in range(PIECES):
             cols = slice(p * PIECE, (p + 1) * PIECE)
             result = ring.tile([P, PIECE], F32, name="result")
-            nc.scalar.activation(result[:], sums[p][:], RELU)
+            if p < last_piece:
+                nc.scalar.activation(result[:], sums[p][:], RELU)
+            else:
+                nc.vector.tensor_scalar_max(result[:], total[:], 0.0)
             nc.sync.dma_start(out[:, cols], result[:])

@@ -36,44 +36,42 @@ def tile_mlpmodel_kernel(tc, table, obs, mask, offs, out):
 
         blocks = {b: held.tile([P, ROBOTS], F32, name=f"block{b}") for b in order}
 
-        mask_small = held.tile([LIMBS * CHUNKS, CHUNK], F32, name="mask_small")
+        mask_small = held.tile([P, CHUNK], F32, name="mask_small")
+        nc.sync.dma_start(mask_small[0 : LIMBS * CHUNKS, :], mask.rearrange("s (c x) -> (s c) x", c=CHUNKS))
+        nc.vector.memset(mask_small[LIMBS * CHUNKS : 64, :], 0.0)
+        nc.vector.memset(mask_small[64:P, :], 0.0)
+        offsets = held.tile([P, N // 16], U16, name="offsets")
+        nc.sync.dma_start(offsets[:], offs)
+        first = order[0]
+        nc.sync.dma_start(blocks[first][:], table[first * P : (first + 1) * P, :])
+
         obs_small = held.tile([LIMBS * CHUNKS, FEATURES, CHUNK], F32, name="obs_small")
-        nc.sync.dma_start(mask_small[:], mask.rearrange("s (c x) -> (s c) x", c=CHUNKS))
         for s in range(LIMBS):
             nc.sync.dma_start(
                 obs_small[s * CHUNKS : (s + 1) * CHUNKS, :, :],
                 obs[s * FEATURES : (s + 1) * FEATURES, :].rearrange("i (c x) -> c i x", c=CHUNKS),
             )
 
-        mask_pieces = held.tile([LIMBS * PIECES, PIECE], F32, name="mask_pieces")
-        nc.sync.dma_start(mask_pieces[:], mask.rearrange("s (p x) -> (s p) x", p=PIECES))
-
-        offsets = held.tile([P, N // 16], U16, name="offsets")
-        nc.sync.dma_start(offsets[:], offs)
-        for b in bias_blocks:
+        for b in bias_blocks[1:]:
             nc.sync.dma_start(blocks[b][:], table[b * P : (b + 1) * P, :])
 
+        pick = held.tile([P, P], BF16, name="pick")
+        make_identity(nc, pick[:])
         identity = held.tile([P, P], F32, name="identity")
         make_identity(nc, identity[:])
 
         warm = held.tile([P, 1], F32, name="warm")
-        nc.scalar.activation(warm[:], identity[:, 0:1], COPY)
-
-        pick = held.tile([P, LIMBS * PIECES], BF16, name="pick")
-        nc.vector.tensor_copy(pick[:], identity[:, 0 : LIMBS * PIECES])
-        keep_pieces = held.tile([P, PIECE], BF16, name="keep_pieces")
-        nc.vector.memset(keep_pieces[:], 0.0)
+        nc.scalar.activation(warm[:], pick[:, 0:1], COPY)
 
         kept_small = held.tile([LIMBS * CHUNKS, FEATURES, CHUNK], F32, name="kept_small")
         nc.vector.scalar_tensor_tensor(
             kept_small[:],
-            mask_small[:].unsqueeze(1).to_broadcast([LIMBS * CHUNKS, FEATURES, CHUNK]),
+            mask_small[0 : LIMBS * CHUNKS, :].unsqueeze(1).to_broadcast([LIMBS * CHUNKS, FEATURES, CHUNK]),
             0.0,
             obs_small[:],
             IS_EQUAL,
             MULT,
         )
-        nc.vector.tensor_scalar(keep_pieces[0 : LIMBS * PIECES, :], mask_pieces[:], -1.0, 1.0, MULT, ADD)
 
         for s in range(LIMBS):
             nc.sync.dma_start(
@@ -85,12 +83,14 @@ def tile_mlpmodel_kernel(tc, table, obs, mask, offs, out):
             nc.sync.dma_start(blocks[b][:], table[b * P : (b + 1) * P, :])
 
         factor = {}
+        mask_halves = mask_small[:].bitcast(BF16)[:, 1::2]
         spread = [psum.tile([P, 2 * PIECE], F32, name=f"spread{t}") for t in range(LIMBS * PIECES // 2)]
-        for q in range(LIMBS * PIECES):
+        per_bank = 2 * PIECE // CHUNK
+        for q in range(LIMBS * CHUNKS):
             nc.tensor.matmul(
-                spread[q // 2][:, (q % 2) * PIECE : (q % 2 + 1) * PIECE],
+                spread[q // per_bank][:, (q % per_bank) * CHUNK : (q % per_bank + 1) * CHUNK],
                 pick[:, q : q + 1].to_broadcast([P, P]),
-                keep_pieces[:],
+                mask_halves,
             )
         for s in range(LIMBS):
             keep = held.tile([P, N], F32, name=f"keep{s}")
@@ -100,6 +100,8 @@ def tile_mlpmodel_kernel(tc, table, obs, mask, offs, out):
                     keep[:, p * PIECE : (p + 1) * PIECE],
                     spread[q // 2][:, (q % 2) * PIECE : (q % 2 + 1) * PIECE],
                     COPY,
+                    bias=1.0,
+                    scale=-1.0,
                 )
             factor[bias_blocks[s]] = keep
         for r, b in enumerate(weight_blocks):

@@ -6,6 +6,7 @@ BF16 = mybir.dt.bfloat16
 U16 = mybir.dt.uint16
 MULT = mybir.AluOpType.mult
 ADD = mybir.AluOpType.add
+SUB = mybir.AluOpType.subtract
 IS_EQUAL = mybir.AluOpType.is_equal
 COPY = mybir.ActivationFunctionType.Copy
 RELU = mybir.ActivationFunctionType.Relu
@@ -21,6 +22,13 @@ PIECES = N // PIECE
 PIECE_COLS = PIECE // 16
 CHUNKS = 16
 CHUNK = N // CHUNKS
+ROWS = LIMBS * CHUNKS
+TERMS = 3
+BANK = 512
+
+
+def upper_half(tile):
+    return tile[:].bitcast(BF16)[:, 1::2]
 
 
 def tile_mlpmodel_kernel(tc, table, obs, mask, offs, out):
@@ -28,7 +36,8 @@ def tile_mlpmodel_kernel(tc, table, obs, mask, offs, out):
     with (
         tc.tile_pool(name="held", bufs=1) as held,
         tc.tile_pool(name="ring", bufs=LIMBS * PER_LIMB * PIECES) as ring,
-        tc.psum_pool(name="psum", bufs=1) as psum,
+        tc.psum_pool(name="totals", bufs=1) as totals,
+        tc.psum_pool(name="passing", bufs=4) as passing,
     ):
         bias_blocks = [PER_LIMB * s + FEATURES for s in range(LIMBS)]
         weight_blocks = [PER_LIMB * s + i for s in range(LIMBS) for i in range(FEATURES)]
@@ -37,22 +46,18 @@ def tile_mlpmodel_kernel(tc, table, obs, mask, offs, out):
         blocks = {b: held.tile([P, ROBOTS], F32, name=f"block{b}") for b in order}
 
         mask_small = held.tile([P, CHUNK], F32, name="mask_small")
-        nc.sync.dma_start(mask_small[0 : LIMBS * CHUNKS, :], mask.rearrange("s (c x) -> (s c) x", c=CHUNKS))
-        nc.vector.memset(mask_small[LIMBS * CHUNKS : 64, :], 0.0)
+        nc.sync.dma_start(mask_small[0:ROWS, :], mask.rearrange("s (c x) -> (s c) x", c=CHUNKS))
+        nc.vector.memset(mask_small[ROWS:64, :], 0.0)
         nc.vector.memset(mask_small[64:P, :], 0.0)
-        offsets = held.tile([P, N // 16], U16, name="offsets")
-        nc.sync.dma_start(offsets[:], offs)
-        first = order[0]
-        nc.sync.dma_start(blocks[first][:], table[first * P : (first + 1) * P, :])
-
-        obs_small = held.tile([LIMBS * CHUNKS, FEATURES, CHUNK], F32, name="obs_small")
+        obs_small = held.tile([ROWS, FEATURES, CHUNK], F32, name="obs_small")
         for s in range(LIMBS):
             nc.sync.dma_start(
                 obs_small[s * CHUNKS : (s + 1) * CHUNKS, :, :],
                 obs[s * FEATURES : (s + 1) * FEATURES, :].rearrange("i (c x) -> c i x", c=CHUNKS),
             )
-
-        for b in bias_blocks[1:]:
+        offsets = held.tile([P, N // 16], U16, name="offsets")
+        nc.sync.dma_start(offsets[:], offs)
+        for b in bias_blocks:
             nc.sync.dma_start(blocks[b][:], table[b * P : (b + 1) * P, :])
 
         pick = held.tile([P, P], BF16, name="pick")
@@ -63,54 +68,92 @@ def tile_mlpmodel_kernel(tc, table, obs, mask, offs, out):
         warm = held.tile([P, 1], F32, name="warm")
         nc.scalar.activation(warm[:], pick[:, 0:1], COPY)
 
-        kept_small = held.tile([LIMBS * CHUNKS, FEATURES, CHUNK], F32, name="kept_small")
+        shift = held.tile([ROWS, (TERMS - 1) * ROWS + P], BF16, name="shift")
+        nc.vector.memset(shift[:], 0.0)
+        nc.vector.tensor_copy(shift[:, (TERMS - 1) * ROWS : TERMS * ROWS], pick[0:ROWS, 0:ROWS])
+        pick_two = held.tile([P, ROWS], BF16, name="pick_two")
+        pick_terms = held.tile([P, ROWS], BF16, name="pick_terms")
+        nc.vector.tensor_tensor(pick_two[:], pick[:, 0:ROWS], pick[:, ROWS : 2 * ROWS], ADD)
+        nc.vector.tensor_tensor(pick_terms[:], pick_two[:], pick[:, 2 * ROWS : 3 * ROWS], ADD)
+
+        kept_small = held.tile([ROWS, FEATURES * CHUNK], F32, name="kept_small")
         nc.vector.scalar_tensor_tensor(
-            kept_small[:],
-            mask_small[0 : LIMBS * CHUNKS, :].unsqueeze(1).to_broadcast([LIMBS * CHUNKS, FEATURES, CHUNK]),
+            kept_small[:].rearrange("q (i x) -> q i x", i=FEATURES),
+            mask_small[0:ROWS, :].unsqueeze(1).to_broadcast([ROWS, FEATURES, CHUNK]),
             0.0,
             obs_small[:],
             IS_EQUAL,
             MULT,
         )
-
-        for s in range(LIMBS):
-            nc.sync.dma_start(
-                out[s * FEATURES : (s + 1) * FEATURES, :].rearrange("i (c x) -> c i x", c=CHUNKS),
-                kept_small[s * CHUNKS : (s + 1) * CHUNKS, :, :],
-            )
-
+        nc.sync.dma_start(
+            out[0:FEATURES, :].rearrange("i (c x) -> c i x", c=CHUNKS),
+            kept_small[CHUNKS:ROWS, :].rearrange("q (i x) -> q i x", i=FEATURES),
+        )
         for b in weight_blocks:
             nc.sync.dma_start(blocks[b][:], table[b * P : (b + 1) * P, :])
 
-        factor = {}
-        mask_halves = mask_small[:].bitcast(BF16)[:, 1::2]
-        spread = [psum.tile([P, 2 * PIECE], F32, name=f"spread{t}") for t in range(LIMBS * PIECES // 2)]
-        per_bank = 2 * PIECE // CHUNK
-        for q in range(LIMBS * CHUNKS):
+        per_bank = BANK // CHUNK
+        spread = [passing.tile([P, BANK], F32, name=f"spread{t}", tag="passing") for t in range(LIMBS * N // BANK)]
+        for q in range(ROWS):
             nc.tensor.matmul(
                 spread[q // per_bank][:, (q % per_bank) * CHUNK : (q % per_bank + 1) * CHUNK],
                 pick[:, q : q + 1].to_broadcast([P, P]),
-                mask_halves,
+                upper_half(mask_small),
             )
+        factor = {}
         for s in range(LIMBS):
             keep = held.tile([P, N], F32, name=f"keep{s}")
             for p in range(PIECES):
-                q = s * PIECES + p
+                at = s * N + p * PIECE
                 nc.scalar.activation(
                     keep[:, p * PIECE : (p + 1) * PIECE],
-                    spread[q // 2][:, (q % 2) * PIECE : (q % 2 + 1) * PIECE],
+                    spread[at // BANK][:, at % BANK : at % BANK + PIECE],
                     COPY,
                     bias=1.0,
                     scale=-1.0,
                 )
-            factor[bias_blocks[s]] = keep
-        for r, b in enumerate(weight_blocks):
-            kept_obs = held.tile([P, N], F32, name=f"kept_obs{r}")
-            nc.sync.dma_start(kept_obs[:], out[r, :].partition_broadcast(P))
-            factor[b] = kept_obs
+            factor[bias_blocks[s]] = keep[:]
+
+        rest = held.tile([ROWS, FEATURES * CHUNK], F32, name="rest")
+        nc.vector.tensor_tensor(rest[:], kept_small[:], upper_half(kept_small), SUB)
+        last_rest = held.tile([ROWS, FEATURES * CHUNK], F32, name="last_rest")
+        nc.vector.tensor_tensor(last_rest[:], rest[:], upper_half(rest), SUB)
+        stacked = passing.tile([P, BANK], F32, name="stacked", tag="passing")
+        for t, part in enumerate([kept_small, rest, last_rest]):
+            nc.tensor.matmul(
+                stacked[:, 0 : FEATURES * CHUNK],
+                shift[:, (TERMS - 1 - t) * ROWS : (TERMS - 1 - t) * ROWS + P],
+                upper_half(part),
+                start=(t == 0),
+                stop=(t == TERMS - 1),
+            )
+        terms = held.tile([P, FEATURES * CHUNK], BF16, name="terms")
+        nc.scalar.activation(terms[:], stacked[:, 0 : FEATURES * CHUNK], COPY)
+
+        kept_obs = held.tile([P, FEATURES, N], F32, name="kept_obs")
+        for c in range(0, CHUNKS, 2):
+            chunks = passing.tile([P, BANK], F32, name="chunks", tag="passing")
+            for e in range(2):
+                nc.tensor.matmul(
+                    chunks[:, e * FEATURES * CHUNK : (e + 1) * FEATURES * CHUNK],
+                    pick_terms[:, c + e : c + e + 1].to_broadcast([P, P]),
+                    terms[:],
+                )
+            nc.scalar.activation(
+                kept_obs[:, :, c * CHUNK : (c + 2) * CHUNK].rearrange("p i (e x) -> p i e x", e=2),
+                chunks[:, 0 : 2 * FEATURES * CHUNK].rearrange("p (e i x) -> p i e x", e=2, i=FEATURES),
+                COPY,
+            )
+        for i in range(FEATURES):
+            factor[i] = kept_obs[:, i, :]
+
+        for i in range(FEATURES):
+            row = held.tile([P, N], F32, name=f"row{i}")
+            nc.sync.dma_start(row[:], out[i, :].partition_broadcast(P))
+            factor[PER_LIMB + i] = row[:]
 
         last_block, last_piece = len(order) - 1, PIECES - 1
-        sums = [psum.tile([P, PIECE], F32, name=f"sum{p}") for p in range(PIECES)]
+        sums = [totals.tile([P, PIECE], F32, name=f"sum{p}") for p in range(PIECES)]
         for k, b in enumerate(order):
             for p in range(PIECES):
                 cols = slice(p * PIECE, (p + 1) * PIECE)

@@ -8,6 +8,7 @@ MULT = mybir.AluOpType.mult
 ADD = mybir.AluOpType.add
 SUB = mybir.AluOpType.subtract
 IS_EQUAL = mybir.AluOpType.is_equal
+NOT_EQUAL = mybir.AluOpType.not_equal
 COPY = mybir.ActivationFunctionType.Copy
 RELU = mybir.ActivationFunctionType.Relu
 
@@ -23,12 +24,14 @@ PIECE_COLS = PIECE // 16
 CHUNKS = 16
 CHUNK = N // CHUNKS
 ROWS = LIMBS * CHUNKS
+FINES = 32
+FINE = N // FINES
 TERMS = 3
 BANK = 512
 
 
-def upper_half(tile):
-    return tile[:].bitcast(BF16)[:, 1::2]
+def upper_half(words):
+    return words.bitcast(BF16)[:, 1::2]
 
 
 def tile_mlpmodel_kernel(tc, table, obs, mask, offs, out):
@@ -49,45 +52,59 @@ def tile_mlpmodel_kernel(tc, table, obs, mask, offs, out):
         nc.sync.dma_start(mask_small[0:ROWS, :], mask.rearrange("s (c x) -> (s c) x", c=CHUNKS))
         nc.vector.memset(mask_small[ROWS:64, :], 0.0)
         nc.vector.memset(mask_small[64:P, :], 0.0)
-        obs_small = held.tile([ROWS, FEATURES, CHUNK], F32, name="obs_small")
+        mask_fine = held.tile([LIMBS * FINES, FINE], F32, name="mask_fine")
+        nc.sync.dma_start(mask_fine[:], mask.rearrange("s (c x) -> (s c) x", c=FINES))
+        obs_fine = held.tile([LIMBS * FINES, FEATURES, FINE], F32, name="obs_fine")
         for s in range(LIMBS):
             nc.sync.dma_start(
-                obs_small[s * CHUNKS : (s + 1) * CHUNKS, :, :],
-                obs[s * FEATURES : (s + 1) * FEATURES, :].rearrange("i (c x) -> c i x", c=CHUNKS),
+                obs_fine[s * FINES : (s + 1) * FINES, :, :],
+                obs[s * FEATURES : (s + 1) * FEATURES, :].rearrange("i (c x) -> c i x", c=FINES),
             )
         offsets = held.tile([P, N // 16], U16, name="offsets")
         nc.sync.dma_start(offsets[:], offs)
         for b in bias_blocks:
             nc.sync.dma_start(blocks[b][:], table[b * P : (b + 1) * P, :])
 
-        pick = held.tile([P, P], BF16, name="pick")
-        make_identity(nc, pick[:])
+        def diagonal(rows, columns, shift, name):
+            tile = held.tile([rows, columns], BF16, name=name)
+            nc.gpsimd.memset(tile[:], 0.0)
+            add_diagonal(tile, shift)
+            return tile
+
+        def add_diagonal(tile, shift):
+            nc.gpsimd.affine_select(
+                out=tile[:],
+                in_=tile[:],
+                compare_op=NOT_EQUAL,
+                fill=1.0,
+                base=-shift,
+                pattern=[[-1, tile.shape[1]]],
+                channel_multiplier=1,
+            )
+
+        pick = diagonal(P, ROWS, 0, "pick")
+        mover = diagonal(FINES, (TERMS - 1) * FINES + P, -(TERMS - 1) * FINES, "mover")
         identity = held.tile([P, P], F32, name="identity")
         make_identity(nc, identity[:])
+        pick_terms = diagonal(P, FINES, 0, "pick_terms")
+        for t in range(1, TERMS):
+            add_diagonal(pick_terms, t * FINES)
 
         warm = held.tile([P, 1], F32, name="warm")
         nc.scalar.activation(warm[:], pick[:, 0:1], COPY)
 
-        shift = held.tile([ROWS, (TERMS - 1) * ROWS + P], BF16, name="shift")
-        nc.vector.memset(shift[:], 0.0)
-        nc.vector.tensor_copy(shift[:, (TERMS - 1) * ROWS : TERMS * ROWS], pick[0:ROWS, 0:ROWS])
-        pick_two = held.tile([P, ROWS], BF16, name="pick_two")
-        pick_terms = held.tile([P, ROWS], BF16, name="pick_terms")
-        nc.vector.tensor_tensor(pick_two[:], pick[:, 0:ROWS], pick[:, ROWS : 2 * ROWS], ADD)
-        nc.vector.tensor_tensor(pick_terms[:], pick_two[:], pick[:, 2 * ROWS : 3 * ROWS], ADD)
-
-        kept_small = held.tile([ROWS, FEATURES * CHUNK], F32, name="kept_small")
+        kept = held.tile([LIMBS * FINES, FEATURES * FINE], F32, name="kept")
         nc.vector.scalar_tensor_tensor(
-            kept_small[:].rearrange("q (i x) -> q i x", i=FEATURES),
-            mask_small[0:ROWS, :].unsqueeze(1).to_broadcast([ROWS, FEATURES, CHUNK]),
+            kept[:].rearrange("q (i x) -> q i x", i=FEATURES),
+            mask_fine[:].unsqueeze(1).to_broadcast([LIMBS * FINES, FEATURES, FINE]),
             0.0,
-            obs_small[:],
+            obs_fine[:],
             IS_EQUAL,
             MULT,
         )
         nc.sync.dma_start(
-            out[0:FEATURES, :].rearrange("i (c x) -> c i x", c=CHUNKS),
-            kept_small[CHUNKS:ROWS, :].rearrange("q (i x) -> q i x", i=FEATURES),
+            out[0:FEATURES, :].rearrange("i (c x) -> c i x", c=FINES),
+            kept[FINES:, :].rearrange("q (i x) -> q i x", i=FEATURES),
         )
         for b in weight_blocks:
             nc.sync.dma_start(blocks[b][:], table[b * P : (b + 1) * P, :])
@@ -98,7 +115,7 @@ def tile_mlpmodel_kernel(tc, table, obs, mask, offs, out):
             nc.tensor.matmul(
                 spread[q // per_bank][:, (q % per_bank) * CHUNK : (q % per_bank + 1) * CHUNK],
                 pick[:, q : q + 1].to_broadcast([P, P]),
-                upper_half(mask_small),
+                upper_half(mask_small[:]),
             )
         factor = {}
         for s in range(LIMBS):
@@ -114,34 +131,35 @@ def tile_mlpmodel_kernel(tc, table, obs, mask, offs, out):
                 )
             factor[bias_blocks[s]] = keep[:]
 
-        rest = held.tile([ROWS, FEATURES * CHUNK], F32, name="rest")
-        nc.vector.tensor_tensor(rest[:], kept_small[:], upper_half(kept_small), SUB)
-        last_rest = held.tile([ROWS, FEATURES * CHUNK], F32, name="last_rest")
-        nc.vector.tensor_tensor(last_rest[:], rest[:], upper_half(rest), SUB)
+        rest = held.tile([FINES, FEATURES * FINE], F32, name="rest")
+        nc.vector.tensor_tensor(rest[:], kept[0:FINES, :], upper_half(kept[0:FINES, :]), SUB)
+        last_rest = held.tile([FINES, FEATURES * FINE], F32, name="last_rest")
+        nc.vector.tensor_tensor(last_rest[:], rest[:], upper_half(rest[:]), SUB)
         stacked = passing.tile([P, BANK], F32, name="stacked", tag="passing")
-        for t, part in enumerate([kept_small, rest, last_rest]):
+        for t, part in enumerate([kept[0:FINES, :], rest[:], last_rest[:]]):
             nc.tensor.matmul(
-                stacked[:, 0 : FEATURES * CHUNK],
-                shift[:, (TERMS - 1 - t) * ROWS : (TERMS - 1 - t) * ROWS + P],
+                stacked[:, 0 : FEATURES * FINE],
+                mover[:, (TERMS - 1 - t) * FINES : (TERMS - 1 - t) * FINES + P],
                 upper_half(part),
                 start=(t == 0),
                 stop=(t == TERMS - 1),
             )
-        terms = held.tile([P, FEATURES * CHUNK], BF16, name="terms")
-        nc.scalar.activation(terms[:], stacked[:, 0 : FEATURES * CHUNK], COPY)
+        terms = held.tile([P, FEATURES * FINE], BF16, name="terms")
+        nc.scalar.activation(terms[:], stacked[:, 0 : FEATURES * FINE], COPY)
 
         kept_obs = held.tile([P, FEATURES, N], F32, name="kept_obs")
-        for c in range(0, CHUNKS, 2):
+        together = PIECE // FINE // 2
+        for c in range(0, FINES, together):
             chunks = passing.tile([P, BANK], F32, name="chunks", tag="passing")
-            for e in range(2):
+            for e in range(together):
                 nc.tensor.matmul(
-                    chunks[:, e * FEATURES * CHUNK : (e + 1) * FEATURES * CHUNK],
+                    chunks[:, e * FEATURES * FINE : (e + 1) * FEATURES * FINE],
                     pick_terms[:, c + e : c + e + 1].to_broadcast([P, P]),
                     terms[:],
                 )
             nc.scalar.activation(
-                kept_obs[:, :, c * CHUNK : (c + 2) * CHUNK].rearrange("p i (e x) -> p i e x", e=2),
-                chunks[:, 0 : 2 * FEATURES * CHUNK].rearrange("p (e i x) -> p i e x", e=2, i=FEATURES),
+                kept_obs[:, :, c * FINE : (c + together) * FINE].rearrange("p i (e x) -> p i e x", e=together),
+                chunks[:, 0 : together * FEATURES * FINE].rearrange("p (e i x) -> p i e x", e=together, i=FEATURES),
                 COPY,
             )
         for i in range(FEATURES):
@@ -152,29 +170,34 @@ def tile_mlpmodel_kernel(tc, table, obs, mask, offs, out):
             nc.sync.dma_start(row[:], out[i, :].partition_broadcast(P))
             factor[PER_LIMB + i] = row[:]
 
-        last_block, last_piece = len(order) - 1, PIECES - 1
+        last_block = len(order) - 1
+        by_vector = [PIECES - 2, PIECES - 1]
         sums = [totals.tile([P, PIECE], F32, name=f"sum{p}") for p in range(PIECES)]
+        last_product = {}
         for k, b in enumerate(order):
             for p in range(PIECES):
                 cols = slice(p * PIECE, (p + 1) * PIECE)
                 piece = offsets[:, p * PIECE_COLS : (p + 1) * PIECE_COLS]
                 product = ring.tile([P, PIECE], F32, name="product")
                 nc.vector.tensor_tensor(product[:], blocks[b][:].indirect(piece), factor[b][:, cols], MULT)
-                if p < last_piece:
-                    nc.tensor.matmul(sums[p][:], identity[:], product[:], start=(k == 0), stop=(k == last_block))
-                elif k < last_block:
-                    nc.tensor.matmul(
-                        sums[p][:], identity[:], product[:], start=(k == 0), stop=(k == last_block - 1)
-                    )
+                closing = last_block - 1 if p in by_vector else last_block
+                if k <= closing:
+                    nc.tensor.matmul(sums[p][:], identity[:], product[:], start=(k == 0), stop=(k == closing))
                 else:
-                    total = ring.tile([P, PIECE], F32, name="total")
-                    nc.vector.tensor_tensor(total[:], product[:], sums[p][:], ADD)
+                    last_product[p] = product
+
+        total = {}
+        for p in by_vector:
+            total[p] = held.tile([P, PIECE], F32, name=f"total{p}")
+            nc.vector.tensor_tensor(total[p][:], last_product[p][:], sums[p][:], ADD)
 
         for p in range(PIECES):
             cols = slice(p * PIECE, (p + 1) * PIECE)
             result = ring.tile([P, PIECE], F32, name="result")
-            if p < last_piece:
-                nc.scalar.activation(result[:], sums[p][:], RELU)
+            if p == PIECES - 1:
+                nc.vector.tensor_scalar_max(result[:], total[p][:], 0.0)
+            elif p in by_vector:
+                nc.scalar.activation(result[:], total[p][:], RELU)
             else:
-                nc.vector.tensor_scalar_max(result[:], total[:], 0.0)
+                nc.scalar.activation(result[:], sums[p][:], RELU)
             nc.sync.dma_start(out[:, cols], result[:])

@@ -120,14 +120,12 @@ def tile_mlpmodel_kernel(tc, table, obs, mask, offs, out):
         factor = {}
         for s in range(LIMBS):
             keep = held.tile([P, N], F32, name=f"keep{s}")
-            for p in range(PIECES):
-                at = s * N + p * PIECE
+            width = PIECE if s == 0 else BANK
+            for at in list(range(0, BANK, width)) + list(range(BANK, N, BANK)):
+                n = width if at < BANK else BANK
+                bank = spread[(s * N + at) // BANK]
                 nc.scalar.activation(
-                    keep[:, p * PIECE : (p + 1) * PIECE],
-                    spread[at // BANK][:, at % BANK : at % BANK + PIECE],
-                    COPY,
-                    bias=1.0,
-                    scale=-1.0,
+                    keep[:, at : at + n], bank[:, at % BANK : at % BANK + n], COPY, bias=1.0, scale=-1.0
                 )
             factor[bias_blocks[s]] = keep[:]
 
@@ -165,10 +163,10 @@ def tile_mlpmodel_kernel(tc, table, obs, mask, offs, out):
         for i in range(FEATURES):
             factor[i] = kept_obs[:, i, :]
 
+        rows = held.tile([P, FEATURES * N], F32, name="rows")
+        nc.sync.dma_start(rows[:], out[0:FEATURES, :].rearrange("i n -> (i n)").partition_broadcast(P))
         for i in range(FEATURES):
-            row = held.tile([P, N], F32, name=f"row{i}")
-            nc.sync.dma_start(row[:], out[i, :].partition_broadcast(P))
-            factor[PER_LIMB + i] = row[:]
+            factor[PER_LIMB + i] = rows[:, i * N : (i + 1) * N]
 
         last_block = len(order) - 1
         by_vector = [PIECES - 2, PIECES - 1]

@@ -168,21 +168,22 @@ def tile_mlpmodel_kernel(tc, table, obs, mask, offs, out):
         for i in range(FEATURES):
             factor[PER_LIMB + i] = rows[:, i * N : (i + 1) * N]
 
-        last_block = len(order) - 1
+        groups = [[b] for b in bias_blocks] + [weight_blocks[:FEATURES]] + [[b] for b in weight_blocks[FEATURES:]]
         by_vector = [PIECES - 2, PIECES - 1]
         sums = [totals.tile([P, PIECE], F32, name=f"sum{p}") for p in range(PIECES)]
         last_product = {}
-        for k, b in enumerate(order):
+        for group in groups:
             for p in range(PIECES):
                 cols = slice(p * PIECE, (p + 1) * PIECE)
                 piece = offsets[:, p * PIECE_COLS : (p + 1) * PIECE_COLS]
-                product = ring.tile([P, PIECE], F32, name="product")
-                nc.vector.tensor_tensor(product[:], blocks[b][:].indirect(piece), factor[b][:, cols], MULT)
-                closing = last_block - 1 if p in by_vector else last_block
-                if k <= closing:
-                    nc.tensor.matmul(sums[p][:], identity[:], product[:], start=(k == 0), stop=(k == closing))
-                else:
-                    last_product[p] = product
+                for b in group:
+                    product = ring.tile([P, PIECE], F32, name="product")
+                    nc.vector.tensor_tensor(product[:], blocks[b][:].indirect(piece), factor[b][:, cols], MULT)
+                    closing = order[-2] if p in by_vector else order[-1]
+                    if b == order[-1] and p in by_vector:
+                        last_product[p] = product
+                    else:
+                        nc.tensor.matmul(sums[p][:], identity[:], product[:], start=(b == order[0]), stop=(b == closing))
 
         total = {}
         for p in by_vector:

@@ -20,7 +20,6 @@ FEATURES = 3
 PER_LIMB = FEATURES + 1
 PIECE = 256
 PIECES = N // PIECE
-PIECE_COLS = PIECE // 16
 CHUNKS = 16
 CHUNK = N // CHUNKS
 ROWS = LIMBS * CHUNKS
@@ -168,35 +167,39 @@ def tile_mlpmodel_kernel(tc, table, obs, mask, offs, out):
         for i in range(FEATURES):
             factor[PER_LIMB + i] = rows[:, i * N : (i + 1) * N]
 
-        groups = [[b] for b in bias_blocks] + [weight_blocks[:FEATURES]] + [[b] for b in weight_blocks[FEATURES:]]
-        by_vector = [PIECES - 2, PIECES - 1]
+        groups = [[b] for b in bias_blocks] + [weight_blocks[:FEATURES], weight_blocks[FEATURES:]]
+        last_piece = PIECES - 1
+        whole, halves = [slice(0, PIECE)], [slice(0, PIECE // 2), slice(PIECE // 2, PIECE)]
         sums = [totals.tile([P, PIECE], F32, name=f"sum{p}") for p in range(PIECES)]
-        last_product = {}
+        last_products = []
         for group in groups:
             for p in range(PIECES):
-                cols = slice(p * PIECE, (p + 1) * PIECE)
-                piece = offsets[:, p * PIECE_COLS : (p + 1) * PIECE_COLS]
                 for b in group:
                     product = ring.tile([P, PIECE], F32, name="product")
-                    nc.vector.tensor_tensor(product[:], blocks[b][:].indirect(piece), factor[b][:, cols], MULT)
-                    closing = order[-2] if p in by_vector else order[-1]
-                    if b == order[-1] and p in by_vector:
-                        last_product[p] = product
+                    for part in halves if (b, p) == (order[-1], last_piece) else whole:
+                        begin, end = p * PIECE + part.start, p * PIECE + part.stop
+                        piece = offsets[:, begin // 16 : end // 16]
+                        nc.vector.tensor_tensor(
+                            product[:, part], blocks[b][:].indirect(piece), factor[b][:, begin:end], MULT
+                        )
+                    if p == last_piece and b in order[-2:]:
+                        last_products.append(product)
                     else:
+                        closing = order[-3] if p == last_piece else order[-1]
                         nc.tensor.matmul(sums[p][:], identity[:], product[:], start=(b == order[0]), stop=(b == closing))
 
-        total = {}
-        for p in by_vector:
-            total[p] = held.tile([P, PIECE], F32, name=f"total{p}")
-            nc.vector.tensor_tensor(total[p][:], last_product[p][:], sums[p][:], ADD)
-
-        for p in range(PIECES):
-            cols = slice(p * PIECE, (p + 1) * PIECE)
+        for p in range(last_piece):
             result = ring.tile([P, PIECE], F32, name="result")
-            if p == PIECES - 1:
-                nc.vector.tensor_scalar_max(result[:], total[p][:], 0.0)
-            elif p in by_vector:
-                nc.scalar.activation(result[:], total[p][:], RELU)
-            else:
-                nc.scalar.activation(result[:], sums[p][:], RELU)
-            nc.sync.dma_start(out[:, cols], result[:])
+            nc.scalar.activation(result[:], sums[p][:], RELU)
+            nc.sync.dma_start(out[:, p * PIECE : (p + 1) * PIECE], result[:])
+
+        pair = ring.tile([P, PIECE], F32, name="pair")
+        total = ring.tile([P, PIECE], F32, name="total")
+        result = ring.tile([P, PIECE], F32, name="result")
+        for part in halves:
+            nc.vector.tensor_tensor(pair[:, part], last_products[0][:, part], last_products[1][:, part], ADD)
+        for part in halves:
+            nc.vector.tensor_tensor(total[:, part], pair[:, part], sums[last_piece][:, part], ADD)
+        for part in halves:
+            nc.vector.tensor_scalar_max(result[:, part], total[:, part], 0.0)
+        nc.sync.dma_start(out[:, last_piece * PIECE :], result[:])

import concourse.mybir as mybir
from concourse.masks import make_identity

F32 = mybir.dt.float32
BF16 = mybir.dt.bfloat16
U16 = mybir.dt.uint16
MULT = mybir.AluOpType.mult
ADD = mybir.AluOpType.add
SUB = mybir.AluOpType.subtract
IS_EQUAL = mybir.AluOpType.is_equal
NOT_EQUAL = mybir.AluOpType.not_equal
COPY = mybir.ActivationFunctionType.Copy
RELU = mybir.ActivationFunctionType.Relu

P = 128
ROBOTS = 256
N = 1024
LIMBS = 2
FEATURES = 3
PER_LIMB = FEATURES + 1
PIECE = 256
PIECES = N // PIECE
CHUNKS = 16
CHUNK = N // CHUNKS
ROWS = LIMBS * CHUNKS
FINES = 32
FINE = N // FINES
TERMS = 3
BANK = 512


def upper_half(words):
    return words.bitcast(BF16)[:, 1::2]


def tile_mlpmodel_kernel(tc, table, obs, mask, offs, out):
    nc = tc.nc
    with (
        tc.tile_pool(name="held", bufs=1) as held,
        tc.tile_pool(name="ring", bufs=LIMBS * PER_LIMB * PIECES) as ring,
        tc.psum_pool(name="totals", bufs=1) as totals,
        tc.psum_pool(name="passing", bufs=4) as passing,
    ):
        bias_blocks = [PER_LIMB * s + FEATURES for s in range(LIMBS)]
        weight_blocks = [PER_LIMB * s + i for s in range(LIMBS) for i in range(FEATURES)]
        order = bias_blocks + weight_blocks

        blocks = {b: held.tile([P, ROBOTS], F32, name=f"block{b}") for b in order}

        mask_small = held.tile([P, CHUNK], F32, name="mask_small")
        nc.sync.dma_start(mask_small[0:ROWS, :], mask.rearrange("s (c x) -> (s c) x", c=CHUNKS))
        nc.vector.memset(mask_small[ROWS:64, :], 0.0)
        nc.vector.memset(mask_small[64:P, :], 0.0)
        mask_fine = held.tile([LIMBS * FINES, FINE], F32, name="mask_fine")
        nc.sync.dma_start(mask_fine[:], mask.rearrange("s (c x) -> (s c) x", c=FINES))
        obs_fine = held.tile([LIMBS * FINES, FEATURES, FINE], F32, name="obs_fine")
        for s in range(LIMBS):
            nc.sync.dma_start(
                obs_fine[s * FINES : (s + 1) * FINES, :, :],
                obs[s * FEATURES : (s + 1) * FEATURES, :].rearrange("i (c x) -> c i x", c=FINES),
            )
        offsets = held.tile([P, N // 16], U16, name="offsets")
        nc.sync.dma_start(offsets[:], offs)
        for b in bias_blocks:
            nc.sync.dma_start(blocks[b][:], table[b * P : (b + 1) * P, :])

        def diagonal(rows, columns, shift, name):
            tile = held.tile([rows, columns], BF16, name=name)
            nc.gpsimd.memset(tile[:], 0.0)
            add_diagonal(tile, shift)
            return tile

        def add_diagonal(tile, shift):
            nc.gpsimd.affine_select(
                out=tile[:],
                in_=tile[:],
                compare_op=NOT_EQUAL,
                fill=1.0,
                base=-shift,
                pattern=[[-1, tile.shape[1]]],
                channel_multiplier=1,
            )

        pick = diagonal(P, ROWS, 0, "pick")
        mover = diagonal(FINES, (TERMS - 1) * FINES + P, -(TERMS - 1) * FINES, "mover")
        identity = held.tile([P, P], F32, name="identity")
        make_identity(nc, identity[:])
        pick_terms = diagonal(P, FINES, 0, "pick_terms")
        for t in range(1, TERMS):
            add_diagonal(pick_terms, t * FINES)

        warm = held.tile([P, 1], F32, name="warm")
        nc.scalar.activation(warm[:], pick[:, 0:1], COPY)

        kept = held.tile([LIMBS * FINES, FEATURES * FINE], F32, name="kept")
        nc.vector.scalar_tensor_tensor(
            kept[:].rearrange("q (i x) -> q i x", i=FEATURES),
            mask_fine[:].unsqueeze(1).to_broadcast([LIMBS * FINES, FEATURES, FINE]),
            0.0,
            obs_fine[:],
            IS_EQUAL,
            MULT,
        )
        nc.sync.dma_start(
            out[0:FEATURES, :].rearrange("i (c x) -> c i x", c=FINES),
            kept[FINES:, :].rearrange("q (i x) -> q i x", i=FEATURES),
        )
        for b in weight_blocks:
            nc.sync.dma_start(blocks[b][:], table[b * P : (b + 1) * P, :])

        per_bank = BANK // CHUNK
        spread = [passing.tile([P, BANK], F32, name=f"spread{t}", tag="passing") for t in range(LIMBS * N // BANK)]
        for q in range(ROWS):
            nc.tensor.matmul(
                spread[q // per_bank][:, (q % per_bank) * CHUNK : (q % per_bank + 1) * CHUNK],
                pick[:, q : q + 1].to_broadcast([P, P]),
                upper_half(mask_small[:]),
            )
        factor = {}
        for s in range(LIMBS):
            keep = held.tile([P, N], F32, name=f"keep{s}")
            width = PIECE if s == 0 else BANK
            for at in list(range(0, BANK, width)) + list(range(BANK, N, BANK)):
                n = width if at < BANK else BANK
                bank = spread[(s * N + at) // BANK]
                nc.scalar.activation(
                    keep[:, at : at + n], bank[:, at % BANK : at % BANK + n], COPY, bias=1.0, scale=-1.0
                )
            factor[bias_blocks[s]] = keep[:]

        rest = held.tile([FINES, FEATURES * FINE], F32, name="rest")
        nc.vector.tensor_tensor(rest[:], kept[0:FINES, :], upper_half(kept[0:FINES, :]), SUB)
        last_rest = held.tile([FINES, FEATURES * FINE], F32, name="last_rest")
        nc.vector.tensor_tensor(last_rest[:], rest[:], upper_half(rest[:]), SUB)
        stacked = passing.tile([P, BANK], F32, name="stacked", tag="passing")
        for t, part in enumerate([kept[0:FINES, :], rest[:], last_rest[:]]):
            nc.tensor.matmul(
                stacked[:, 0 : FEATURES * FINE],
                mover[:, (TERMS - 1 - t) * FINES : (TERMS - 1 - t) * FINES + P],
                upper_half(part),
                start=(t == 0),
                stop=(t == TERMS - 1),
            )
        terms = held.tile([P, FEATURES * FINE], BF16, name="terms")
        nc.scalar.activation(terms[:], stacked[:, 0 : FEATURES * FINE], COPY)

        kept_obs = held.tile([P, FEATURES, N], F32, name="kept_obs")
        together = PIECE // FINE // 2
        for c in range(0, FINES, together):
            chunks = passing.tile([P, BANK], F32, name="chunks", tag="passing")
            for e in range(together):
                nc.tensor.matmul(
                    chunks[:, e * FEATURES * FINE : (e + 1) * FEATURES * FINE],
                    pick_terms[:, c + e : c + e + 1].to_broadcast([P, P]),
                    terms[:],
                )
            nc.scalar.activation(
                kept_obs[:, :, c * FINE : (c + together) * FINE].rearrange("p i (e x) -> p i e x", e=together),
                chunks[:, 0 : together * FEATURES * FINE].rearrange("p (e i x) -> p i e x", e=together, i=FEATURES),
                COPY,
            )
        for i in range(FEATURES):
            factor[i] = kept_obs[:, i, :]

        rows = held.tile([P, FEATURES * N], F32, name="rows")
        nc.sync.dma_start(rows[:], out[0:FEATURES, :].rearrange("i n -> (i n)").partition_broadcast(P))
        for i in range(FEATURES):
            factor[PER_LIMB + i] = rows[:, i * N : (i + 1) * N]

        groups = [[b] for b in bias_blocks] + [weight_blocks[:FEATURES], weight_blocks[FEATURES:]]
        last_piece = PIECES - 1
        whole, halves = [slice(0, PIECE)], [slice(0, PIECE // 2), slice(PIECE // 2, PIECE)]
        sums = [totals.tile([P, PIECE], F32, name=f"sum{p}") for p in range(PIECES)]
        last_products = []
        for group in groups:
            for p in range(PIECES):
                for b in group:
                    product = ring.tile([P, PIECE], F32, name="product")
                    for part in halves if (b, p) == (order[-1], last_piece) else whole:
                        begin, end = p * PIECE + part.start, p * PIECE + part.stop
                        piece = offsets[:, begin // 16 : end // 16]
                        nc.vector.tensor_tensor(
                            product[:, part], blocks[b][:].indirect(piece), factor[b][:, begin:end], MULT
                        )
                    if p == last_piece and b in order[-2:]:
                        last_products.append(product)
                    else:
                        closing = order[-3] if p == last_piece else order[-1]
                        nc.tensor.matmul(sums[p][:], identity[:], product[:], start=(b == order[0]), stop=(b == closing))

        for p in range(last_piece):
            result = ring.tile([P, PIECE], F32, name="result")
            nc.scalar.activation(result[:], sums[p][:], RELU)
            nc.sync.dma_start(out[:, p * PIECE : (p + 1) * PIECE], result[:])

        pair = ring.tile([P, PIECE], F32, name="pair")
        total = ring.tile([P, PIECE], F32, name="total")
        result = ring.tile([P, PIECE], F32, name="result")
        for part in halves:
            nc.vector.tensor_tensor(pair[:, part], last_products[0][:, part], last_products[1][:, part], ADD)
        for part in halves:
            nc.vector.tensor_tensor(total[:, part], pair[:, part], sums[last_piece][:, part], ADD)
        for part in halves:
            nc.vector.tensor_scalar_max(result[:, part], total[:, part], 0.0)
        nc.sync.dma_start(out[:, last_piece * PIECE :], result[:])
